import numpy as np
import ml_dtypes


def mxq(x, axis, fmt="e4m3"):
    dtype, down = {"e4m3": (ml_dtypes.float8_e4m3fn, 7), "e5m2": (ml_dtypes.float8_e5m2, 14)}[fmt]
    v = np.moveaxis(np.asarray(x, np.float32).astype(ml_dtypes.bfloat16).astype(np.float64), axis, -1)
    blocks = v.reshape(v.shape[:-1] + (-1, 32))
    amax = np.abs(blocks).max(-1, keepdims=True)
    byte = np.maximum(np.where(amax > 0, np.frexp(amax)[1] - 1 + 127, 0) - down, 1)
    scale = np.exp2(byte - 127.0)
    codes = (blocks / scale).astype(np.float32).astype(dtype).astype(np.float64)
    return np.moveaxis((codes * scale).reshape(v.shape), -1, axis)


WIDE = False


def mx_kscale(k):
    if not WIDE:
        return np.ones(k)
    levels = np.array([10, -10, 5, -5, 0])
    a = np.random.permutation(np.resize(levels, k // 512 * 4)).reshape(k // 512, 4)
    idx = np.arange(k)
    return np.exp2(a[idx // 512, idx % 128 // 32])


BF16 = ml_dtypes.bfloat16


def bf(x):
    return np.asarray(x, np.float32).astype(BF16)


def f64(x):
    return np.asarray(x).astype(np.float64)


B, DIM, D2, T = 32, 512, 512, 128


def setup_inputs():
    s = mx_kscale(D2)
    es = 0.25 * s[None, :, None]
    ws = 0.35 / np.sqrt(D2) / s[:, None] / s[None, :]
    return {"E_re": bf(np.random.standard_normal((B, D2, T)) * es),
            "E_im": bf(np.random.standard_normal((B, D2, T)) * es),
            "WKQ_re": bf(np.random.standard_normal((D2, D2)) * ws),
            "WKQ_im": bf(np.random.standard_normal((D2, D2)) * ws)}


def reference(E_re, E_im, WKQ_re, WKQ_im):
    er = mxq(f64(E_re), 1, "e4m3")
    ei = mxq(f64(E_im), 1, "e4m3")
    wr = mxq(f64(WKQ_re), 1, "e4m3")
    wi = mxq(f64(WKQ_im), 1, "e4m3")
    q_re = (wr @ er) - (wi @ ei)
    q_im = (wr @ ei) + (wi @ er)
    qr = mxq(q_re, 1, "e4m3")
    qi = mxq(q_im, 1, "e4m3")
    ert = er.transpose(0, 2, 1)
    eit = ei.transpose(0, 2, 1)
    s_re = (ert @ qr) + (eit @ qi)
    s_im = (ert @ qi) - (eit @ qr)
    return s_re, s_im

@@ -1,0 +1,221 @@
+from contextlib import ExitStack
+
+import concourse.mybir as mybir
+from concourse.masks import make_identity
+
+F32 = mybir.dt.float32
+BF16 = mybir.dt.bfloat16
+U32 = mybir.dt.uint32
+U8 = mybir.dt.uint8
+FP8X4 = mybir.dt.float8_e4m3fn_x4
+
+P = 128
+PACK = 4
+B = 32
+D = 512
+T = 128
+RE = 0
+IM = 1
+NEG_IM = 2
+
+FLOPS = 2 * B * (4 * D * D * T + 4 * T * D * T)
+
+LOAD_CHUNKS = [1, 1, 2, 2, 2, 4, 4, 4, 4, 4, 4]
+STORE_GROUPS = [4, 4, 4, 4, 4, 4, 4, 2, 1, 1]
+REGROUP_AHEAD = 3
+QUANT_AHEAD = 2
+S2_LAG = 2
+
+
+def tile_autoregressivelsa_pa_t_kernel(tc, E_re, E_im, WKQ_re, WKQ_im, out_0, out_1):
+    nc = tc.nc
+    assert sum(LOAD_CHUNKS) == B and sum(STORE_GROUPS) == B
+    with ExitStack() as ctx:
+        keep = ctx.enter_context(tc.tile_pool(name="keep", bufs=1))
+        rot = ctx.enter_context(tc.tile_pool(name="rot", bufs=4))
+        outs = ctx.enter_context(tc.tile_pool(name="outs", bufs=3))
+        pq = ctx.enter_context(tc.psum_pool(name="pq", bufs=4))
+        ps = ctx.enter_context(tc.psum_pool(name="ps", bufs=4))
+        ctx.enter_context(tc.manual_schedule())
+
+        w_dram = [WKQ_re, WKQ_im]
+        w_raw = []
+        for m in range(2):
+            wr = keep.tile([P, PACK * D], BF16, name="w_raw%d" % m)
+            nc.sync.dma_start(out=wr[:], in_=w_dram[m].rearrange("(p j) c -> p (j c)", j=PACK))
+            w_raw.append(wr)
+        where = {}
+        b0 = 0
+        for k, n in enumerate(LOAD_CHUNKS):
+            er = keep.tile([P, 2, n, PACK * T], BF16, name="e_raw%d" % k)
+            nc.sync.dma_start(out=er[:, RE, :, :], in_=E_re[b0:b0 + n].rearrange("b (p j) t -> p b (j t)", j=PACK))
+            nc.sync.dma_start(out=er[:, IM, :, :], in_=E_im[b0:b0 + n].rearrange("b (p j) t -> p b (j t)", j=PACK))
+            for bb in range(n):
+                where[b0 + bb] = (er, bb)
+            b0 += n
+
+        ident = keep.tile([P, P], F32, name="ident")
+        make_identity(nc, ident[:])
+
+        w_grp = [keep.tile([P, PACK * D], BF16, name="w_grp%d" % m, align_bytes=64) for m in range(3)]
+        w_codes = [keep.tile([P, D], U32, name="w_codes%d" % m, align_bytes=64) for m in range(3)]
+        w_scales = [keep.tile([P, D], U8, name="w_scales%d" % m, align_bytes=64) for m in range(3)]
+        e_codes = [keep.tile([P, 2 * T], U32, name="e_codes%d" % b, align_bytes=64) for b in range(B)]
+        e_scales = [keep.tile([P, 2 * T], U8, name="e_scales%d" % b, align_bytes=64) for b in range(B)]
+
+        e_grp = {}
+        q_bank = {}
+        q_grp = {}
+        q_codes = {}
+        q_scales = {}
+        s_bank = {}
+        group_of = {}
+        b0 = 0
+        for g, n in enumerate(STORE_GROUPS):
+            for bb in range(n):
+                group_of[b0 + bb] = (g, bb, n, b0)
+            b0 += n
+        xz_tiles = {}
+        oim_tiles = {}
+
+        def w_transpose_and_copy(m, h):
+            words = w_raw[m][:].bitcast(F32).rearrange("p (j q e) -> p j e q", j=PACK, e=2)
+            bank = pq.tile([P, 2, 2, P], F32, name="w_bank", tag="q")
+            for e in range(2):
+                for jj in range(2):
+                    nc.tensor.transpose(bank[:, e, jj, :], words[:, 2 * h + jj, e, :], ident[:])
+            nc.scalar.copy(
+                out=w_grp[m][:, h * 1024:(h + 1) * 1024].bitcast(F32).rearrange("p (c e) -> p c e", e=2),
+                in_=bank[:].rearrange("p e jj q -> p (jj q) e"),
+            )
+
+        def w_negate(h):
+            nc.vector.tensor_scalar_mul(
+                out=w_grp[NEG_IM][:, h * 1024:(h + 1) * 1024],
+                in0=w_grp[IM][:, h * 1024:(h + 1) * 1024],
+                scalar1=-1.0,
+            )
+
+        def w_quantise(m):
+            nc.vector.quantize_mx(out=w_codes[m][:].bitcast(FP8X4), scales=w_scales[m][:], in_=w_grp[m][:])
+
+        def regroup(b):
+            if b >= B:
+                return
+            er, bb = where[b]
+            eg = rot.tile([P, 2, T, PACK], BF16, name="e_grp", tag="e_grp", align_bytes=64)
+            nc.vector.tensor_copy(
+                out=eg[:].rearrange("p a (c i) j -> p a c j i", i=4),
+                in_=er[:, :, bb, :].rearrange("p a (j c i) -> p a c j i", j=PACK, i=4),
+            )
+            e_grp[b] = eg
+
+        def e_quantise(b):
+            if b >= B:
+                return
+            nc.vector.quantize_mx(
+                out=e_codes[b][:].bitcast(FP8X4),
+                scales=e_scales[b][:],
+                in_=e_grp[b][:].rearrange("p a t j -> p (a t j)"),
+            )
+
+        def cols(a):
+            return slice(a * T, (a + 1) * T)
+
+        def stage1(b, part):
+            if part == RE:
+                terms = [(RE, RE), (NEG_IM, IM)]
+            else:
+                terms = [(RE, IM), (IM, RE)]
+            bank = pq.tile([P, PACK, T], F32, name="q_bank", tag="q")
+            for j in range(PACK):
+                for n, (m, a) in enumerate(terms):
+                    nc.tensor.matmul_mx(
+                        out=bank[:, j, :],
+                        lhsT=w_codes[m][:, cols(j)].bitcast(FP8X4),
+                        lhsT_scale=w_scales[m][:, cols(j)],
+                        rhs=e_codes[b][:, cols(a)].bitcast(FP8X4),
+                        rhs_scale=e_scales[b][:, cols(a)],
+                        start=(n == 0),
+                        stop=(n == 1),
+                    )
+            q_bank[(b, part)] = bank
+
+        def q_out(b, part):
+            if b not in q_grp:
+                q_grp[b] = rot.tile([P, 2, T, PACK], BF16, name="q_grp", tag="q_grp", align_bytes=64)
+            nc.scalar.copy(out=q_grp[b][:, part, :, :], in_=q_bank[(b, part)][:].rearrange("p j t -> p t j"))
+
+        def q_quantise(b):
+            if b < 0 or b >= B:
+                return
+            q_codes[b] = rot.tile([P, 2 * T], U32, name="q_codes", tag="q_codes", align_bytes=64)
+            q_scales[b] = rot.tile([P, 2 * T], U8, name="q_scales", tag="q_scales", align_bytes=64)
+            nc.vector.quantize_mx(
+                out=q_codes[b][:].bitcast(FP8X4),
+                scales=q_scales[b][:],
+                in_=q_grp[b][:].rearrange("p a t j -> p (a t j)"),
+            )
+
+        def stage2(b):
+            if b < 0 or b >= B:
+                return
+            bank = ps.tile([P, 3, T], F32, name="s_bank", tag="s")
+            passes = [(0, RE, RE, True, False), (0, IM, IM, False, True), (1, IM, RE, True, True), (2, RE, IM, True, True)]
+            for slot, a, q, first, last in passes:
+                nc.tensor.matmul_mx(
+                    out=bank[:, slot, :],
+                    lhsT=e_codes[b][:, cols(a)].bitcast(FP8X4),
+                    lhsT_scale=e_scales[b][:, cols(a)],
+                    rhs=q_codes[b][:, cols(q)].bitcast(FP8X4),
+                    rhs_scale=q_scales[b][:, cols(q)],
+                    start=first,
+                    stop=last,
+                )
+            s_bank[b] = bank
+
+        def s_out(b):
+            if b < 0 or b >= B:
+                return
+            g, bb, n, first_b = group_of[b]
+            if bb == 0:
+                xz_tiles[g] = outs.tile([P, 2, n, T], F32, name="xz", tag="xz")
+                oim_tiles[g] = outs.tile([P, n, T], F32, name="oim", tag="oim")
+            nc.scalar.copy(out=xz_tiles[g][:, :, bb, :], in_=s_bank[b][:, 0:2, :])
+
+        def s_sub_and_store(b):
+            if b < 0 or b >= B:
+                return
+            g, bb, n, first_b = group_of[b]
+            nc.vector.tensor_sub(out=oim_tiles[g][:, bb, :], in0=s_bank[b][:, 2, :], in1=xz_tiles[g][:, 1, bb, :])
+            if bb == n - 1:
+                nc.sync.dma_start(out=out_0[first_b:first_b + n].rearrange("b i j -> i b j"), in_=xz_tiles[g][:, 0, :, :])
+                nc.sync.dma_start(out=out_1[first_b:first_b + n].rearrange("b i j -> i b j"), in_=oim_tiles[g][:])
+
+        w_transpose_and_copy(RE, 0)
+        w_transpose_and_copy(RE, 1)
+        regroup(0)
+        w_quantise(RE)
+        w_transpose_and_copy(IM, 0)
+        w_transpose_and_copy(IM, 1)
+        e_quantise(0)
+        regroup(1)
+        w_negate(0)
+        w_quantise(IM)
+        w_negate(1)
+        e_quantise(1)
+        w_quantise(NEG_IM)
+        regroup(2)
+
+        for i in range(B + S2_LAG + 1):
+            q_quantise(i - 1)
+            if i < B:
+                stage1(i, IM)
+                q_out(i, IM)
+                stage1(i, RE)
+                q_out(i, RE)
+            regroup(i + REGROUP_AHEAD)
+            stage2(i - S2_LAG)
+            s_out(i - S2_LAG)
+            s_sub_and_store(i - S2_LAG - 1)
+            e_quantise(i + QUANT_AHEAD)

@@ -38,6 +38,14 @@ def tile_autoregressivelsa_pa_t_kernel(tc, E_re, E_im, WKQ_re, WKQ_im, out_0, ou
         ps = ctx.enter_context(tc.psum_pool(name="ps", bufs=4))
         ctx.enter_context(tc.manual_schedule())
 
+        warm = keep.tile([P, 512], BF16, name="warm")
+        nc.vector.memset(warm[:], 0.0)
+        warm_bank = ps.tile([P, 512], F32, name="warm_bank", tag="s")
+
+        def keep_clock_up(count):
+            for r in range(count):
+                nc.tensor.matmul(out=warm_bank[:], lhsT=warm[:, 0:P], rhs=warm[:], start=True, stop=True)
+
         w_dram = [WKQ_re, WKQ_im]
         w_raw = []
         for m in range(2):
@@ -192,12 +200,15 @@ def tile_autoregressivelsa_pa_t_kernel(tc, E_re, E_im, WKQ_re, WKQ_im, out_0, ou
                 nc.sync.dma_start(out=out_0[first_b:first_b + n].rearrange("b i j -> i b j"), in_=xz_tiles[g][:, 0, :, :])
                 nc.sync.dma_start(out=out_1[first_b:first_b + n].rearrange("b i j -> i b j"), in_=oim_tiles[g][:])
 
+        keep_clock_up(10)
         w_transpose_and_copy(RE, 0)
         w_transpose_and_copy(RE, 1)
+        keep_clock_up(2)
         regroup(0)
         w_quantise(RE)
         w_transpose_and_copy(IM, 0)
         w_transpose_and_copy(IM, 1)
+        keep_clock_up(4)
         e_quantise(0)
         regroup(1)
         w_negate(0)

@@ -25,6 +25,8 @@ STORE_GROUPS = [4, 4, 4, 4, 4, 4, 4, 2, 1, 1]
 REGROUP_AHEAD = 3
 QUANT_AHEAD = 2
 S2_LAG = 2
+VECTOR_HELPS_FROM = 28
+SCALAR_REGROUPS = (1,)
 
 
 def tile_autoregressivelsa_pa_t_kernel(tc, E_re, E_im, WKQ_re, WKQ_im, out_0, out_1):
@@ -33,43 +35,54 @@ def tile_autoregressivelsa_pa_t_kernel(tc, E_re, E_im, WKQ_re, WKQ_im, out_0, ou
     with ExitStack() as ctx:
         keep = ctx.enter_context(tc.tile_pool(name="keep", bufs=1))
         rot = ctx.enter_context(tc.tile_pool(name="rot", bufs=4))
+        qrot = ctx.enter_context(tc.tile_pool(name="qrot", bufs=S2_LAG + 3))
         outs = ctx.enter_context(tc.tile_pool(name="outs", bufs=3))
         pq = ctx.enter_context(tc.psum_pool(name="pq", bufs=4))
         ps = ctx.enter_context(tc.psum_pool(name="ps", bufs=4))
         ctx.enter_context(tc.manual_schedule())
 
-        warm = keep.tile([P, 512], BF16, name="warm")
-        nc.vector.memset(warm[:], 0.0)
-        warm_bank = ps.tile([P, 512], F32, name="warm_bank", tag="s")
-
-        def keep_clock_up(count):
-            for r in range(count):
-                nc.tensor.matmul(out=warm_bank[:], lhsT=warm[:, 0:P], rhs=warm[:], start=True, stop=True)
-
         w_dram = [WKQ_re, WKQ_im]
-        w_raw = []
-        for m in range(2):
-            wr = keep.tile([P, PACK * D], BF16, name="w_raw%d" % m)
-            nc.sync.dma_start(out=wr[:], in_=w_dram[m].rearrange("(p j) c -> p (j c)", j=PACK))
-            w_raw.append(wr)
+        w_raw = {}
+        w_grp = {}
+        w_codes = {}
+        w_scales = {}
+        for m in range(3):
+            for h in range(2):
+                if m != NEG_IM:
+                    w_raw[(m, h)] = keep.tile([P, 2 * D], BF16, name="w_raw%d%d" % (m, h))
+                w_grp[(m, h)] = keep.tile([P, 2 * D], BF16, name="w_grp%d%d" % (m, h), align_bytes=64)
+                w_codes[(m, h)] = keep.tile([P, 2 * P], U32, name="w_codes%d%d" % (m, h), align_bytes=64)
+                w_scales[(m, h)] = keep.tile([P, 2 * P], U8, name="w_scales%d%d" % (m, h), align_bytes=64)
+        e_codes = [keep.tile([P, 2 * T], U32, name="e_codes%d" % b, align_bytes=64) for b in range(B)]
+        e_scales = [keep.tile([P, 2 * T], U8, name="e_scales%d" % b, align_bytes=64) for b in range(B)]
         where = {}
-        b0 = 0
-        for k, n in enumerate(LOAD_CHUNKS):
+        chunk_start = [sum(LOAD_CHUNKS[:k]) for k in range(len(LOAD_CHUNKS))]
+
+        def load_w(m, h):
+            nc.sync.dma_start(
+                out=w_raw[(m, h)][:].rearrange("p (j c) -> p j c", j=2),
+                in_=w_dram[m].rearrange("(p j) c -> p j c", j=PACK)[:, 2 * h:2 * h + 2, :],
+            )
+
+        def load_e(k):
+            n = LOAD_CHUNKS[k]
+            b0 = chunk_start[k]
             er = keep.tile([P, 2, n, PACK * T], BF16, name="e_raw%d" % k)
             nc.sync.dma_start(out=er[:, RE, :, :], in_=E_re[b0:b0 + n].rearrange("b (p j) t -> p b (j t)", j=PACK))
             nc.sync.dma_start(out=er[:, IM, :, :], in_=E_im[b0:b0 + n].rearrange("b (p j) t -> p b (j t)", j=PACK))
             for bb in range(n):
                 where[b0 + bb] = (er, bb)
-            b0 += n
+
+        load_w(RE, 0)
+        load_w(IM, 0)
+        load_e(0)
+        load_w(RE, 1)
+        load_w(IM, 1)
+        for k in range(1, len(LOAD_CHUNKS)):
+            load_e(k)
 
         ident = keep.tile([P, P], F32, name="ident")
         make_identity(nc, ident[:])
-
-        w_grp = [keep.tile([P, PACK * D], BF16, name="w_grp%d" % m, align_bytes=64) for m in range(3)]
-        w_codes = [keep.tile([P, D], U32, name="w_codes%d" % m, align_bytes=64) for m in range(3)]
-        w_scales = [keep.tile([P, D], U8, name="w_scales%d" % m, align_bytes=64) for m in range(3)]
-        e_codes = [keep.tile([P, 2 * T], U32, name="e_codes%d" % b, align_bytes=64) for b in range(B)]
-        e_scales = [keep.tile([P, 2 * T], U8, name="e_scales%d" % b, align_bytes=64) for b in range(B)]
 
         e_grp = {}
         q_bank = {}
@@ -87,36 +100,39 @@ def tile_autoregressivelsa_pa_t_kernel(tc, E_re, E_im, WKQ_re, WKQ_im, out_0, ou
         oim_tiles = {}
 
         def w_transpose_and_copy(m, h):
-            words = w_raw[m][:].bitcast(F32).rearrange("p (j q e) -> p j e q", j=PACK, e=2)
+            words = w_raw[(m, h)][:].bitcast(F32).rearrange("p (j q e) -> p j e q", j=2, e=2)
             bank = pq.tile([P, 2, 2, P], F32, name="w_bank", tag="q")
             for e in range(2):
                 for jj in range(2):
-                    nc.tensor.transpose(bank[:, e, jj, :], words[:, 2 * h + jj, e, :], ident[:])
+                    nc.tensor.transpose(bank[:, e, jj, :], words[:, jj, e, :], ident[:])
             nc.scalar.copy(
-                out=w_grp[m][:, h * 1024:(h + 1) * 1024].bitcast(F32).rearrange("p (c e) -> p c e", e=2),
+                out=w_grp[(m, h)][:].bitcast(F32).rearrange("p (c e) -> p c e", e=2),
                 in_=bank[:].rearrange("p e jj q -> p (jj q) e"),
             )
 
         def w_negate(h):
-            nc.vector.tensor_scalar_mul(
-                out=w_grp[NEG_IM][:, h * 1024:(h + 1) * 1024],
-                in0=w_grp[IM][:, h * 1024:(h + 1) * 1024],
-                scalar1=-1.0,
-            )
+            nc.vector.tensor_scalar_mul(out=w_grp[(NEG_IM, h)][:], in0=w_grp[(IM, h)][:], scalar1=-1.0)
 
-        def w_quantise(m):
-            nc.vector.quantize_mx(out=w_codes[m][:].bitcast(FP8X4), scales=w_scales[m][:], in_=w_grp[m][:])
+        def w_quantise(m, h):
+            nc.vector.quantize_mx(out=w_codes[(m, h)][:].bitcast(FP8X4), scales=w_scales[(m, h)][:], in_=w_grp[(m, h)][:])
 
         def regroup(b):
             if b >= B:
                 return
             er, bb = where[b]
             eg = rot.tile([P, 2, T, PACK], BF16, name="e_grp", tag="e_grp", align_bytes=64)
-            nc.vector.tensor_copy(
-                out=eg[:].rearrange("p a (c i) j -> p a c j i", i=4),
-                in_=er[:, :, bb, :].rearrange("p a (j c i) -> p a c j i", j=PACK, i=4),
-            )
             e_grp[b] = eg
+            if b in SCALAR_REGROUPS:
+                for a in range(2):
+                    nc.scalar.copy(
+                        out=eg[:, a, :, :].rearrange("p (c i) j -> p c j i", i=4),
+                        in_=er[:, a, bb, :].rearrange("p (j c i) -> p c j i", j=PACK, i=4),
+                    )
+            else:
+                nc.vector.tensor_copy(
+                    out=eg[:].rearrange("p a (c i) j -> p a c j i", i=4),
+                    in_=er[:, :, bb, :].rearrange("p a (j c i) -> p a c j i", j=PACK, i=4),
+                )
 
         def e_quantise(b):
             if b >= B:
@@ -130,35 +146,38 @@ def tile_autoregressivelsa_pa_t_kernel(tc, E_re, E_im, WKQ_re, WKQ_im, out_0, ou
         def cols(a):
             return slice(a * T, (a + 1) * T)
 
-        def stage1(b, part):
+        def stage1(b, part, h):
             if part == RE:
                 terms = [(RE, RE), (NEG_IM, IM)]
             else:
                 terms = [(RE, IM), (IM, RE)]
-            bank = pq.tile([P, PACK, T], F32, name="q_bank", tag="q")
-            for j in range(PACK):
+            if h == 0:
+                q_bank[(b, part)] = pq.tile([P, PACK, T], F32, name="q_bank", tag="q")
+            for jj in range(2):
                 for n, (m, a) in enumerate(terms):
                     nc.tensor.matmul_mx(
-                        out=bank[:, j, :],
-                        lhsT=w_codes[m][:, cols(j)].bitcast(FP8X4),
-                        lhsT_scale=w_scales[m][:, cols(j)],
+                        out=q_bank[(b, part)][:, 2 * h + jj, :],
+                        lhsT=w_codes[(m, h)][:, cols(jj)].bitcast(FP8X4),
+                        lhsT_scale=w_scales[(m, h)][:, cols(jj)],
                         rhs=e_codes[b][:, cols(a)].bitcast(FP8X4),
                         rhs_scale=e_scales[b][:, cols(a)],
                         start=(n == 0),
                         stop=(n == 1),
                     )
-            q_bank[(b, part)] = bank
 
         def q_out(b, part):
             if b not in q_grp:
                 q_grp[b] = rot.tile([P, 2, T, PACK], BF16, name="q_grp", tag="q_grp", align_bytes=64)
-            nc.scalar.copy(out=q_grp[b][:, part, :, :], in_=q_bank[(b, part)][:].rearrange("p j t -> p t j"))
+            if part == RE and b >= VECTOR_HELPS_FROM:
+                nc.vector.tensor_copy(out=q_grp[b][:, part, :, :], in_=q_bank[(b, part)][:].rearrange("p j t -> p t j"))
+            else:
+                nc.scalar.copy(out=q_grp[b][:, part, :, :], in_=q_bank[(b, part)][:].rearrange("p j t -> p t j"))
 
         def q_quantise(b):
             if b < 0 or b >= B:
                 return
-            q_codes[b] = rot.tile([P, 2 * T], U32, name="q_codes", tag="q_codes", align_bytes=64)
-            q_scales[b] = rot.tile([P, 2 * T], U8, name="q_scales", tag="q_scales", align_bytes=64)
+            q_codes[b] = qrot.tile([P, 2 * T], U32, name="q_codes", tag="q_codes", align_bytes=64)
+            q_scales[b] = qrot.tile([P, 2 * T], U8, name="q_scales", tag="q_scales", align_bytes=64)
             nc.vector.quantize_mx(
                 out=q_codes[b][:].bitcast(FP8X4),
                 scales=q_scales[b][:],
@@ -200,30 +219,32 @@ def tile_autoregressivelsa_pa_t_kernel(tc, E_re, E_im, WKQ_re, WKQ_im, out_0, ou
                 nc.sync.dma_start(out=out_0[first_b:first_b + n].rearrange("b i j -> i b j"), in_=xz_tiles[g][:, 0, :, :])
                 nc.sync.dma_start(out=out_1[first_b:first_b + n].rearrange("b i j -> i b j"), in_=oim_tiles[g][:])
 
-        keep_clock_up(10)
         w_transpose_and_copy(RE, 0)
-        w_transpose_and_copy(RE, 1)
-        keep_clock_up(2)
-        regroup(0)
-        w_quantise(RE)
+        w_quantise(RE, 0)
         w_transpose_and_copy(IM, 0)
-        w_transpose_and_copy(IM, 1)
-        keep_clock_up(4)
+        regroup(0)
+        w_quantise(IM, 0)
         e_quantise(0)
-        regroup(1)
         w_negate(0)
-        w_quantise(IM)
+        w_quantise(NEG_IM, 0)
+        w_transpose_and_copy(RE, 1)
+        w_quantise(RE, 1)
+        w_transpose_and_copy(IM, 1)
+        w_quantise(IM, 1)
         w_negate(1)
+        w_quantise(NEG_IM, 1)
+        regroup(1)
         e_quantise(1)
-        w_quantise(NEG_IM)
         regroup(2)
 
         for i in range(B + S2_LAG + 1):
             q_quantise(i - 1)
             if i < B:
-                stage1(i, IM)
+                stage1(i, IM, 0)
+                stage1(i, RE, 0)
+                stage1(i, IM, 1)
                 q_out(i, IM)
-                stage1(i, RE)
+                stage1(i, RE, 1)
                 q_out(i, RE)
             regroup(i + REGROUP_AHEAD)
             stage2(i - S2_LAG)

@@ -24,8 +24,8 @@ LOAD_CHUNKS = [1, 1, 2, 2, 2, 4, 4, 4, 4, 4, 4]
 STORE_GROUPS = [4, 4, 4, 4, 4, 4, 4, 2, 1, 1]
 REGROUP_AHEAD = 3
 QUANT_AHEAD = 2
-S2_LAG = 2
-VECTOR_HELPS_FROM = 28
+S2_LAG = 4
+VECTOR_HELPS_FROM = 30
 SCALAR_REGROUPS = (1,)
 
 

@@ -36,7 +36,7 @@ def tile_autoregressivelsa_pa_t_kernel(tc, E_re, E_im, WKQ_re, WKQ_im, out_0, ou
         keep = ctx.enter_context(tc.tile_pool(name="keep", bufs=1))
         rot = ctx.enter_context(tc.tile_pool(name="rot", bufs=4))
         qrot = ctx.enter_context(tc.tile_pool(name="qrot", bufs=S2_LAG + 3))
-        outs = ctx.enter_context(tc.tile_pool(name="outs", bufs=3))
+        outs = ctx.enter_context(tc.tile_pool(name="outs", bufs=6))
         pq = ctx.enter_context(tc.psum_pool(name="pq", bufs=4))
         ps = ctx.enter_context(tc.psum_pool(name="ps", bufs=4))
         ctx.enter_context(tc.manual_schedule())

@@ -22,6 +22,7 @@ FLOPS = 2 * B * (4 * D * D * T + 4 * T * D * T)
 
 LOAD_CHUNKS = [1, 1, 2, 2, 2, 4, 4, 4, 4, 4, 4]
 STORE_GROUPS = [4, 4, 4, 4, 4, 4, 4, 2, 1, 1]
+GROUPS = [1] * 4 + [2] * 13 + [1] * 2
 REGROUP_AHEAD = 3
 QUANT_AHEAD = 2
 S2_LAG = 4
@@ -31,7 +32,16 @@ SCALAR_REGROUPS = (1,)
 
 def tile_autoregressivelsa_pa_t_kernel(tc, E_re, E_im, WKQ_re, WKQ_im, out_0, out_1):
     nc = tc.nc
-    assert sum(LOAD_CHUNKS) == B and sum(STORE_GROUPS) == B
+    assert sum(LOAD_CHUNKS) == B and sum(STORE_GROUPS) == B and sum(GROUPS) == B
+    starts = {}
+    ends = {}
+    member = {}
+    for g, n in enumerate(GROUPS):
+        first_b = sum(GROUPS[:g])
+        starts[first_b] = g
+        ends[first_b + n - 1] = g
+        for bb in range(n):
+            member[first_b + bb] = (g, bb)
     with ExitStack() as ctx:
         keep = ctx.enter_context(tc.tile_pool(name="keep", bufs=1))
         rot = ctx.enter_context(tc.tile_pool(name="rot", bufs=4))
@@ -53,8 +63,8 @@ def tile_autoregressivelsa_pa_t_kernel(tc, E_re, E_im, WKQ_re, WKQ_im, out_0, ou
                 w_grp[(m, h)] = keep.tile([P, 2 * D], BF16, name="w_grp%d%d" % (m, h), align_bytes=64)
                 w_codes[(m, h)] = keep.tile([P, 2 * P], U32, name="w_codes%d%d" % (m, h), align_bytes=64)
                 w_scales[(m, h)] = keep.tile([P, 2 * P], U8, name="w_scales%d%d" % (m, h), align_bytes=64)
-        e_codes = [keep.tile([P, 2 * T], U32, name="e_codes%d" % b, align_bytes=64) for b in range(B)]
-        e_scales = [keep.tile([P, 2 * T], U8, name="e_scales%d" % b, align_bytes=64) for b in range(B)]
+        e_codes = [keep.tile([P, 2 * n * T], U32, name="e_codes%d" % g, align_bytes=64) for g, n in enumerate(GROUPS)]
+        e_scales = [keep.tile([P, 2 * n * T], U8, name="e_scales%d" % g, align_bytes=64) for g, n in enumerate(GROUPS)]
         where = {}
         chunk_start = [sum(LOAD_CHUNKS[:k]) for k in range(len(LOAD_CHUNKS))]
 
@@ -67,9 +77,9 @@ def tile_autoregressivelsa_pa_t_kernel(tc, E_re, E_im, WKQ_re, WKQ_im, out_0, ou
         def load_e(k):
             n = LOAD_CHUNKS[k]
             b0 = chunk_start[k]
-            er = keep.tile([P, 2, n, PACK * T], BF16, name="e_raw%d" % k)
-            nc.sync.dma_start(out=er[:, RE, :, :], in_=E_re[b0:b0 + n].rearrange("b (p j) t -> p b (j t)", j=PACK))
-            nc.sync.dma_start(out=er[:, IM, :, :], in_=E_im[b0:b0 + n].rearrange("b (p j) t -> p b (j t)", j=PACK))
+            er = keep.tile([P, n, 2, PACK * T], BF16, name="e_raw%d" % k)
+            nc.sync.dma_start(out=er[:, :, RE, :], in_=E_re[b0:b0 + n].rearrange("b (p j) t -> p b (j t)", j=PACK))
+            nc.sync.dma_start(out=er[:, :, IM, :], in_=E_im[b0:b0 + n].rearrange("b (p j) t -> p b (j t)", j=PACK))
             for bb in range(n):
                 where[b0 + bb] = (er, bb)
 
@@ -117,30 +127,33 @@ def tile_autoregressivelsa_pa_t_kernel(tc, E_re, E_im, WKQ_re, WKQ_im, out_0, ou
             nc.vector.quantize_mx(out=w_codes[(m, h)][:].bitcast(FP8X4), scales=w_scales[(m, h)][:], in_=w_grp[(m, h)][:])
 
         def regroup(b):
-            if b >= B:
+            if b not in starts:
                 return
+            g = starts[b]
+            n = GROUPS[g]
             er, bb = where[b]
-            eg = rot.tile([P, 2, T, PACK], BF16, name="e_grp", tag="e_grp", align_bytes=64)
-            e_grp[b] = eg
-            if b in SCALAR_REGROUPS:
-                for a in range(2):
+            eg = rot.tile([P, 2 * n, T, PACK], BF16, name="e_grp", tag="e_grp", align_bytes=64)
+            e_grp[g] = eg
+            if g in SCALAR_REGROUPS:
+                for a in range(2 * n):
                     nc.scalar.copy(
                         out=eg[:, a, :, :].rearrange("p (c i) j -> p c j i", i=4),
-                        in_=er[:, a, bb, :].rearrange("p (j c i) -> p c j i", j=PACK, i=4),
+                        in_=er[:, bb + a // 2, a % 2, :].rearrange("p (j c i) -> p c j i", j=PACK, i=4),
                     )
             else:
                 nc.vector.tensor_copy(
-                    out=eg[:].rearrange("p a (c i) j -> p a c j i", i=4),
-                    in_=er[:, :, bb, :].rearrange("p a (j c i) -> p a c j i", j=PACK, i=4),
+                    out=eg[:].rearrange("p u (c i) j -> p u c j i", i=4),
+                    in_=er[:, bb:bb + n, :, :].rearrange("p b a (j c i) -> p (b a) c j i", j=PACK, i=4),
                 )
 
         def e_quantise(b):
-            if b >= B:
+            if b not in starts:
                 return
+            g = starts[b]
             nc.vector.quantize_mx(
-                out=e_codes[b][:].bitcast(FP8X4),
-                scales=e_scales[b][:],
-                in_=e_grp[b][:].rearrange("p a t j -> p (a t j)"),
+                out=e_codes[g][:].bitcast(FP8X4),
+                scales=e_scales[g][:],
+                in_=e_grp[g][:].rearrange("p u t j -> p (u t j)"),
             )
 
         def cols(a):
@@ -151,6 +164,7 @@ def tile_autoregressivelsa_pa_t_kernel(tc, E_re, E_im, WKQ_re, WKQ_im, out_0, ou
                 terms = [(RE, RE), (NEG_IM, IM)]
             else:
                 terms = [(RE, IM), (IM, RE)]
+            g, bb = member[b]
             if h == 0:
                 q_bank[(b, part)] = pq.tile([P, PACK, T], F32, name="q_bank", tag="q")
             for jj in range(2):
@@ -159,43 +173,47 @@ def tile_autoregressivelsa_pa_t_kernel(tc, E_re, E_im, WKQ_re, WKQ_im, out_0, ou
                         out=q_bank[(b, part)][:, 2 * h + jj, :],
                         lhsT=w_codes[(m, h)][:, cols(jj)].bitcast(FP8X4),
                         lhsT_scale=w_scales[(m, h)][:, cols(jj)],
-                        rhs=e_codes[b][:, cols(a)].bitcast(FP8X4),
-                        rhs_scale=e_scales[b][:, cols(a)],
+                        rhs=e_codes[g][:, cols(2 * bb + a)].bitcast(FP8X4),
+                        rhs_scale=e_scales[g][:, cols(2 * bb + a)],
                         start=(n == 0),
                         stop=(n == 1),
                     )
 
         def q_out(b, part):
-            if b not in q_grp:
-                q_grp[b] = rot.tile([P, 2, T, PACK], BF16, name="q_grp", tag="q_grp", align_bytes=64)
+            g, bb = member[b]
+            if g not in q_grp:
+                q_grp[g] = rot.tile([P, 2 * GROUPS[g], T, PACK], BF16, name="q_grp", tag="q_grp", align_bytes=64)
             if part == RE and b >= VECTOR_HELPS_FROM:
-                nc.vector.tensor_copy(out=q_grp[b][:, part, :, :], in_=q_bank[(b, part)][:].rearrange("p j t -> p t j"))
+                nc.vector.tensor_copy(out=q_grp[g][:, 2 * bb + part, :, :], in_=q_bank[(b, part)][:].rearrange("p j t -> p t j"))
             else:
-                nc.scalar.copy(out=q_grp[b][:, part, :, :], in_=q_bank[(b, part)][:].rearrange("p j t -> p t j"))
+                nc.scalar.copy(out=q_grp[g][:, 2 * bb + part, :, :], in_=q_bank[(b, part)][:].rearrange("p j t -> p t j"))
 
         def q_quantise(b):
-            if b < 0 or b >= B:
+            if b not in ends:
                 return
-            q_codes[b] = qrot.tile([P, 2 * T], U32, name="q_codes", tag="q_codes", align_bytes=64)
-            q_scales[b] = qrot.tile([P, 2 * T], U8, name="q_scales", tag="q_scales", align_bytes=64)
+            g = ends[b]
+            n = GROUPS[g]
+            q_codes[g] = qrot.tile([P, 2 * n * T], U32, name="q_codes", tag="q_codes", align_bytes=64)
+            q_scales[g] = qrot.tile([P, 2 * n * T], U8, name="q_scales", tag="q_scales", align_bytes=64)
             nc.vector.quantize_mx(
-                out=q_codes[b][:].bitcast(FP8X4),
-                scales=q_scales[b][:],
-                in_=q_grp[b][:].rearrange("p a t j -> p (a t j)"),
+                out=q_codes[g][:].bitcast(FP8X4),
+                scales=q_scales[g][:],
+                in_=q_grp[g][:].rearrange("p u t j -> p (u t j)"),
             )
 
         def stage2(b):
             if b < 0 or b >= B:
                 return
+            g, bb = member[b]
             bank = ps.tile([P, 3, T], F32, name="s_bank", tag="s")
             passes = [(0, RE, RE, True, False), (0, IM, IM, False, True), (1, IM, RE, True, True), (2, RE, IM, True, True)]
             for slot, a, q, first, last in passes:
                 nc.tensor.matmul_mx(
                     out=bank[:, slot, :],
-                    lhsT=e_codes[b][:, cols(a)].bitcast(FP8X4),
-                    lhsT_scale=e_scales[b][:, cols(a)],
-                    rhs=q_codes[b][:, cols(q)].bitcast(FP8X4),
-                    rhs_scale=q_scales[b][:, cols(q)],
+                    lhsT=e_codes[g][:, cols(2 * bb + a)].bitcast(FP8X4),
+                    lhsT_scale=e_scales[g][:, cols(2 * bb + a)],
+                    rhs=q_codes[g][:, cols(2 * bb + q)].bitcast(FP8X4),
+                    rhs_scale=q_scales[g][:, cols(2 * bb + q)],
                     start=first,
                     stop=last,
                 )

@@ -252,8 +252,11 @@ def tile_autoregressivelsa_pa_t_kernel(tc, E_re, E_im, WKQ_re, WKQ_im, out_0, ou
         w_negate(1)
         w_quantise(NEG_IM, 1)
         regroup(1)
-        e_quantise(1)
         regroup(2)
+        e_quantise(1)
+        regroup(3)
+        e_quantise(2)
+        e_quantise(3)
 
         for i in range(B + S2_LAG + 1):
             q_quantise(i - 1)
@@ -264,8 +267,10 @@ def tile_autoregressivelsa_pa_t_kernel(tc, E_re, E_im, WKQ_re, WKQ_im, out_0, ou
                 q_out(i, IM)
                 stage1(i, RE, 1)
                 q_out(i, RE)
-            regroup(i + REGROUP_AHEAD)
+            if i > 0:
+                regroup(i + REGROUP_AHEAD)
             stage2(i - S2_LAG)
             s_out(i - S2_LAG)
             s_sub_and_store(i - S2_LAG - 1)
-            e_quantise(i + QUANT_AHEAD)
+            if i > 1:
+                e_quantise(i + QUANT_AHEAD)

@@ -206,14 +206,15 @@ def tile_autoregressivelsa_pa_t_kernel(tc, E_re, E_im, WKQ_re, WKQ_im, out_0, ou
                 return
             g, bb = member[b]
             bank = ps.tile([P, 3, T], F32, name="s_bank", tag="s")
-            passes = [(0, RE, RE, True, False), (0, IM, IM, False, True), (1, IM, RE, True, True), (2, RE, IM, True, True)]
-            for slot, a, q, first, last in passes:
+            passes = [(1, RE, RE, 2, True, False), (1, IM, IM, 1, False, True), (0, IM, RE, 1, True, True)]
+            for slot, a, q, n, first, last in passes:
+                q_cols = slice((2 * bb + q) * T, (2 * bb + q + n) * T)
                 nc.tensor.matmul_mx(
-                    out=bank[:, slot, :],
+                    out=bank[:, slot:slot + n, :].rearrange("p s t -> p (s t)"),
                     lhsT=e_codes[g][:, cols(2 * bb + a)].bitcast(FP8X4),
                     lhsT_scale=e_scales[g][:, cols(2 * bb + a)],
-                    rhs=q_codes[g][:, cols(2 * bb + q)].bitcast(FP8X4),
-                    rhs_scale=q_scales[g][:, cols(2 * bb + q)],
+                    rhs=q_codes[g][:, q_cols].bitcast(FP8X4),
+                    rhs_scale=q_scales[g][:, q_cols],
                     start=first,
                     stop=last,
                 )
@@ -232,9 +233,9 @@ def tile_autoregressivelsa_pa_t_kernel(tc, E_re, E_im, WKQ_re, WKQ_im, out_0, ou
             if b < 0 or b >= B:
                 return
             g, bb, n, first_b = group_of[b]
-            nc.vector.tensor_sub(out=oim_tiles[g][:, bb, :], in0=s_bank[b][:, 2, :], in1=xz_tiles[g][:, 1, bb, :])
+            nc.vector.tensor_sub(out=oim_tiles[g][:, bb, :], in0=s_bank[b][:, 2, :], in1=xz_tiles[g][:, 0, bb, :])
             if bb == n - 1:
-                nc.sync.dma_start(out=out_0[first_b:first_b + n].rearrange("b i j -> i b j"), in_=xz_tiles[g][:, 0, :, :])
+                nc.sync.dma_start(out=out_0[first_b:first_b + n].rearrange("b i j -> i b j"), in_=xz_tiles[g][:, 1, :, :])
                 nc.sync.dma_start(out=out_1[first_b:first_b + n].rearrange("b i j -> i b j"), in_=oim_tiles[g][:])
 
         w_transpose_and_copy(RE, 0)

@@ -20,14 +20,15 @@ NEG_IM = 2
 
 FLOPS = 2 * B * (4 * D * D * T + 4 * T * D * T)
 
-LOAD_CHUNKS = [1, 1, 2, 2, 2, 4, 4, 4, 4, 4, 4]
+LOAD_CHUNKS = [1, 1, 1, 1, 2, 2, 4, 4, 4, 4, 4, 4]
 STORE_GROUPS = [4, 4, 4, 4, 4, 4, 4, 2, 1, 1]
 GROUPS = [1] * 4 + [2] * 13 + [1] * 2
 REGROUP_AHEAD = 3
 QUANT_AHEAD = 2
 S2_LAG = 4
 VECTOR_HELPS_FROM = 30
-SCALAR_REGROUPS = (1,)
+SCALAR_REGROUPS = (2,)
+HEAD_BATCHES = 2
 
 
 def tile_autoregressivelsa_pa_t_kernel(tc, E_re, E_im, WKQ_re, WKQ_im, out_0, out_1):
@@ -84,11 +85,12 @@ def tile_autoregressivelsa_pa_t_kernel(tc, E_re, E_im, WKQ_re, WKQ_im, out_0, ou
                 where[b0 + bb] = (er, bb)
 
         load_w(RE, 0)
-        load_w(IM, 0)
         load_e(0)
+        load_w(IM, 0)
+        load_e(1)
         load_w(RE, 1)
         load_w(IM, 1)
-        for k in range(1, len(LOAD_CHUNKS)):
+        for k in range(2, len(LOAD_CHUNKS)):
             load_e(k)
 
         ident = keep.tile([P, P], F32, name="ident")
@@ -111,7 +113,7 @@ def tile_autoregressivelsa_pa_t_kernel(tc, E_re, E_im, WKQ_re, WKQ_im, out_0, ou
 
         def w_transpose_and_copy(m, h):
             words = w_raw[(m, h)][:].bitcast(F32).rearrange("p (j q e) -> p j e q", j=2, e=2)
-            bank = pq.tile([P, 2, 2, P], F32, name="w_bank", tag="q")
+            bank = ps.tile([P, 2, 2, P], F32, name="w_bank", tag="s")
             for e in range(2):
                 for jj in range(2):
                     nc.tensor.transpose(bank[:, e, jj, :], words[:, jj, e, :], ident[:])
@@ -159,14 +161,16 @@ def tile_autoregressivelsa_pa_t_kernel(tc, E_re, E_im, WKQ_re, WKQ_im, out_0, ou
         def cols(a):
             return slice(a * T, (a + 1) * T)
 
+        def new_q_banks(b):
+            for part in (IM, RE):
+                q_bank[(b, part)] = pq.tile([P, PACK, T], F32, name="q_bank", tag="q")
+
         def stage1(b, part, h):
             if part == RE:
                 terms = [(RE, RE), (NEG_IM, IM)]
             else:
                 terms = [(RE, IM), (IM, RE)]
             g, bb = member[b]
-            if h == 0:
-                q_bank[(b, part)] = pq.tile([P, PACK, T], F32, name="q_bank", tag="q")
             for jj in range(2):
                 for n, (m, a) in enumerate(terms):
                     nc.tensor.matmul_mx(
@@ -238,38 +242,47 @@ def tile_autoregressivelsa_pa_t_kernel(tc, E_re, E_im, WKQ_re, WKQ_im, out_0, ou
                 nc.sync.dma_start(out=out_0[first_b:first_b + n].rearrange("b i j -> i b j"), in_=xz_tiles[g][:, 1, :, :])
                 nc.sync.dma_start(out=out_1[first_b:first_b + n].rearrange("b i j -> i b j"), in_=oim_tiles[g][:])
 
+        regroup(0)
         w_transpose_and_copy(RE, 0)
         w_quantise(RE, 0)
-        w_transpose_and_copy(IM, 0)
-        regroup(0)
-        w_quantise(IM, 0)
         e_quantise(0)
+        regroup(1)
+        w_transpose_and_copy(IM, 0)
         w_negate(0)
+        w_quantise(IM, 0)
+        e_quantise(1)
         w_quantise(NEG_IM, 0)
         w_transpose_and_copy(RE, 1)
         w_quantise(RE, 1)
         w_transpose_and_copy(IM, 1)
-        w_quantise(IM, 1)
         w_negate(1)
+        w_quantise(IM, 1)
         w_quantise(NEG_IM, 1)
-        regroup(1)
         regroup(2)
-        e_quantise(1)
+        for b in range(HEAD_BATCHES):
+            new_q_banks(b)
+        for h in range(2):
+            for part in (IM, RE):
+                for b in range(HEAD_BATCHES):
+                    stage1(b, part, h)
+        for b in range(HEAD_BATCHES):
+            q_out(b, IM)
+            q_out(b, RE)
         regroup(3)
         e_quantise(2)
         e_quantise(3)
 
-        for i in range(B + S2_LAG + 1):
+        for i in range(1, B + S2_LAG + 1):
             q_quantise(i - 1)
-            if i < B:
+            if HEAD_BATCHES <= i < B:
+                new_q_banks(i)
                 stage1(i, IM, 0)
                 stage1(i, RE, 0)
                 stage1(i, IM, 1)
                 q_out(i, IM)
                 stage1(i, RE, 1)
                 q_out(i, RE)
-            if i > 0:
-                regroup(i + REGROUP_AHEAD)
+            regroup(i + REGROUP_AHEAD)
             stage2(i - S2_LAG)
             s_out(i - S2_LAG)
             s_sub_and_store(i - S2_LAG - 1)

@@ -93,8 +93,15 @@ def tile_autoregressivelsa_pa_t_kernel(tc, E_re, E_im, WKQ_re, WKQ_im, out_0, ou
         for k in range(2, len(LOAD_CHUNKS)):
             load_e(k)
 
+        zeros = keep.tile([P, 4 * T], BF16, name="zeros")
+        nc.vector.memset(zeros[:], 0.0)
         ident = keep.tile([P, P], F32, name="ident")
         make_identity(nc, ident[:])
+        warm_bank = pq.tile([P, 4 * T], F32, name="warm_bank", tag="q")
+
+        def warm(n):
+            for k in range(n):
+                nc.tensor.matmul(warm_bank[:], zeros[:, 0:P], zeros[:], start=True, stop=True)
 
         e_grp = {}
         q_bank = {}
@@ -243,16 +250,20 @@ def tile_autoregressivelsa_pa_t_kernel(tc, E_re, E_im, WKQ_re, WKQ_im, out_0, ou
                 nc.sync.dma_start(out=out_1[first_b:first_b + n].rearrange("b i j -> i b j"), in_=oim_tiles[g][:])
 
         regroup(0)
+        warm(5)
         w_transpose_and_copy(RE, 0)
+        warm(2)
         w_quantise(RE, 0)
         e_quantise(0)
         regroup(1)
         w_transpose_and_copy(IM, 0)
+        warm(1)
         w_negate(0)
         w_quantise(IM, 0)
         e_quantise(1)
         w_quantise(NEG_IM, 0)
         w_transpose_and_copy(RE, 1)
+        warm(1)
         w_quantise(RE, 1)
         w_transpose_and_copy(IM, 1)
         w_negate(1)

@@ -21,7 +21,7 @@ NEG_IM = 2
 FLOPS = 2 * B * (4 * D * D * T + 4 * T * D * T)
 
 LOAD_CHUNKS = [1, 1, 1, 1, 2, 2, 4, 4, 4, 4, 4, 4]
-STORE_GROUPS = [4, 4, 4, 4, 4, 4, 4, 2, 1, 1]
+STORE_GROUPS = [4, 4, 4, 4, 4, 4, 2, 2, 2, 1, 1]
 GROUPS = [1] * 4 + [2] * 13 + [1] * 2
 REGROUP_AHEAD = 3
 QUANT_AHEAD = 2
@@ -29,6 +29,8 @@ S2_LAG = 4
 VECTOR_HELPS_FROM = 30
 SCALAR_REGROUPS = (2,)
 HEAD_BATCHES = 2
+HALVES = ((0, 1), (2, 3))
+W_PIECES = (HALVES, HALVES, HALVES)
 
 
 def tile_autoregressivelsa_pa_t_kernel(tc, E_re, E_im, WKQ_re, WKQ_im, out_0, out_1):
@@ -57,22 +59,27 @@ def tile_autoregressivelsa_pa_t_kernel(tc, E_re, E_im, WKQ_re, WKQ_im, out_0, ou
         w_grp = {}
         w_codes = {}
         w_scales = {}
+        w_of = {}
         for m in range(3):
-            for h in range(2):
+            for h, js in enumerate(W_PIECES[m]):
+                n = len(js)
                 if m != NEG_IM:
-                    w_raw[(m, h)] = keep.tile([P, 2 * D], BF16, name="w_raw%d%d" % (m, h))
-                w_grp[(m, h)] = keep.tile([P, 2 * D], BF16, name="w_grp%d%d" % (m, h), align_bytes=64)
-                w_codes[(m, h)] = keep.tile([P, 2 * P], U32, name="w_codes%d%d" % (m, h), align_bytes=64)
-                w_scales[(m, h)] = keep.tile([P, 2 * P], U8, name="w_scales%d%d" % (m, h), align_bytes=64)
+                    w_raw[(m, h)] = keep.tile([P, n * D], BF16, name="w_raw%d%d" % (m, h))
+                w_grp[(m, h)] = keep.tile([P, n * D], BF16, name="w_grp%d%d" % (m, h), align_bytes=64)
+                w_codes[(m, h)] = keep.tile([P, n * P], U32, name="w_codes%d%d" % (m, h), align_bytes=64)
+                w_scales[(m, h)] = keep.tile([P, n * P], U8, name="w_scales%d%d" % (m, h), align_bytes=64)
+                for jj, j in enumerate(js):
+                    w_of[(m, j)] = (h, jj)
         e_codes = [keep.tile([P, 2 * n * T], U32, name="e_codes%d" % g, align_bytes=64) for g, n in enumerate(GROUPS)]
         e_scales = [keep.tile([P, 2 * n * T], U8, name="e_scales%d" % g, align_bytes=64) for g, n in enumerate(GROUPS)]
         where = {}
         chunk_start = [sum(LOAD_CHUNKS[:k]) for k in range(len(LOAD_CHUNKS))]
 
         def load_w(m, h):
+            js = W_PIECES[m][h]
             nc.sync.dma_start(
-                out=w_raw[(m, h)][:].rearrange("p (j c) -> p j c", j=2),
-                in_=w_dram[m].rearrange("(p j) c -> p j c", j=PACK)[:, 2 * h:2 * h + 2, :],
+                out=w_raw[(m, h)][:].rearrange("p (j c) -> p j c", j=len(js)),
+                in_=w_dram[m].rearrange("(p j) c -> p j c", j=PACK)[:, js[0]:js[0] + len(js), :],
             )
 
         def load_e(k):
@@ -92,12 +99,11 @@ def tile_autoregressivelsa_pa_t_kernel(tc, E_re, E_im, WKQ_re, WKQ_im, out_0, ou
         load_w(IM, 1)
         for k in range(2, len(LOAD_CHUNKS)):
             load_e(k)
-
-        zeros = keep.tile([P, 4 * T], BF16, name="zeros")
+        zeros = keep.tile([P, 2 * T], BF16, name="zeros")
         nc.vector.memset(zeros[:], 0.0)
         ident = keep.tile([P, P], F32, name="ident")
         make_identity(nc, ident[:])
-        warm_bank = pq.tile([P, 4 * T], F32, name="warm_bank", tag="q")
+        warm_bank = pq.tile([P, 2 * T], F32, name="warm_bank", tag="q")
 
         def warm(n):
             for k in range(n):
@@ -119,10 +125,11 @@ def tile_autoregressivelsa_pa_t_kernel(tc, E_re, E_im, WKQ_re, WKQ_im, out_0, ou
         oim_tiles = {}
 
         def w_transpose_and_copy(m, h):
-            words = w_raw[(m, h)][:].bitcast(F32).rearrange("p (j q e) -> p j e q", j=2, e=2)
-            bank = ps.tile([P, 2, 2, P], F32, name="w_bank", tag="s")
+            n = len(W_PIECES[m][h])
+            words = w_raw[(m, h)][:].bitcast(F32).rearrange("p (j q e) -> p j e q", j=n, e=2)
+            bank = ps.tile([P, 2, n, P], F32, name="w_bank", tag="s")
             for e in range(2):
-                for jj in range(2):
+                for jj in range(n):
                     nc.tensor.transpose(bank[:, e, jj, :], words[:, jj, e, :], ident[:])
             nc.scalar.copy(
                 out=w_grp[(m, h)][:].bitcast(F32).rearrange("p (c e) -> p c e", e=2),
@@ -172,16 +179,17 @@ def tile_autoregressivelsa_pa_t_kernel(tc, E_re, E_im, WKQ_re, WKQ_im, out_0, ou
             for part in (IM, RE):
                 q_bank[(b, part)] = pq.tile([P, PACK, T], F32, name="q_bank", tag="q")
 
-        def stage1(b, part, h):
+        def stage1(b, part, js):
             if part == RE:
                 terms = [(RE, RE), (NEG_IM, IM)]
             else:
                 terms = [(RE, IM), (IM, RE)]
             g, bb = member[b]
-            for jj in range(2):
+            for j in js:
                 for n, (m, a) in enumerate(terms):
+                    h, jj = w_of[(m, j)]
                     nc.tensor.matmul_mx(
-                        out=q_bank[(b, part)][:, 2 * h + jj, :],
+                        out=q_bank[(b, part)][:, j, :],
                         lhsT=w_codes[(m, h)][:, cols(jj)].bitcast(FP8X4),
                         lhsT_scale=w_scales[(m, h)][:, cols(jj)],
                         rhs=e_codes[g][:, cols(2 * bb + a)].bitcast(FP8X4),
@@ -211,6 +219,43 @@ def tile_autoregressivelsa_pa_t_kernel(tc, E_re, E_im, WKQ_re, WKQ_im, out_0, ou
                 scales=q_scales[g][:],
                 in_=q_grp[g][:].rearrange("p u t j -> p (u t j)"),
             )
+
+        def q_quantise_part(b, part):
+            g, bb = member[b]
+            n = GROUPS[g]
+            if g not in q_codes:
+                q_codes[g] = qrot.tile([P, 2 * n * T], U32, name="q_codes", tag="q_codes", align_bytes=64)
+                q_scales[g] = qrot.tile([P, 2 * n * T], U8, name="q_scales", tag="q_scales", align_bytes=64)
+            part_cols = cols(2 * bb + part)
+            nc.vector.quantize_mx(
+                out=q_codes[g][:, part_cols].bitcast(FP8X4),
+                scales=q_scales[g][:, part_cols],
+                in_=q_grp[g][:, 2 * bb + part, :, :].rearrange("p t j -> p (t j)"),
+            )
+
+        def stage2_last(b):
+            g, bb = member[b]
+            sg, sbb, n, first_b = group_of[b]
+            xz = outs.tile([P, 2, n, T], F32, name="xz", tag="xz")
+            oim = outs.tile([P, n, T], F32, name="oim", tag="oim")
+            banks = {}
+            for slot, a, q, first, last_pass in [(0, IM, RE, True, True), (2, RE, IM, True, True), (1, RE, RE, True, False), (1, IM, IM, False, True)]:
+                if first:
+                    banks[slot] = pq.tile([P, T], F32, name="last_bank", tag="q")
+                nc.tensor.matmul_mx(
+                    out=banks[slot][:],
+                    lhsT=e_codes[g][:, cols(2 * bb + a)].bitcast(FP8X4),
+                    lhsT_scale=e_scales[g][:, cols(2 * bb + a)],
+                    rhs=q_codes[g][:, cols(2 * bb + q)].bitcast(FP8X4),
+                    rhs_scale=q_scales[g][:, cols(2 * bb + q)],
+                    start=first,
+                    stop=last_pass,
+                )
+            nc.scalar.copy(out=xz[:, 0, 0, :], in_=banks[0][:])
+            nc.scalar.copy(out=xz[:, 1, 0, :], in_=banks[1][:])
+            nc.vector.tensor_sub(out=oim[:, 0, :], in0=banks[2][:], in1=xz[:, 0, 0, :])
+            nc.sync.dma_start(out=out_0[first_b:first_b + n].rearrange("b i j -> i b j"), in_=xz[:, 1, :, :])
+            nc.sync.dma_start(out=out_1[first_b:first_b + n].rearrange("b i j -> i b j"), in_=oim[:])
 
         def stage2(b):
             if b < 0 or b >= B:
@@ -250,20 +295,20 @@ def tile_autoregressivelsa_pa_t_kernel(tc, E_re, E_im, WKQ_re, WKQ_im, out_0, ou
                 nc.sync.dma_start(out=out_1[first_b:first_b + n].rearrange("b i j -> i b j"), in_=oim_tiles[g][:])
 
         regroup(0)
-        warm(5)
+        warm(8)
         w_transpose_and_copy(RE, 0)
         warm(2)
         w_quantise(RE, 0)
         e_quantise(0)
         regroup(1)
         w_transpose_and_copy(IM, 0)
-        warm(1)
+        warm(2)
         w_negate(0)
         w_quantise(IM, 0)
         e_quantise(1)
         w_quantise(NEG_IM, 0)
         w_transpose_and_copy(RE, 1)
-        warm(1)
+        warm(2)
         w_quantise(RE, 1)
         w_transpose_and_copy(IM, 1)
         w_negate(1)
@@ -272,26 +317,25 @@ def tile_autoregressivelsa_pa_t_kernel(tc, E_re, E_im, WKQ_re, WKQ_im, out_0, ou
         regroup(2)
         for b in range(HEAD_BATCHES):
             new_q_banks(b)
-        for h in range(2):
+        for js in HALVES:
             for part in (IM, RE):
                 for b in range(HEAD_BATCHES):
-                    stage1(b, part, h)
+                    stage1(b, part, js)
         for b in range(HEAD_BATCHES):
             q_out(b, IM)
             q_out(b, RE)
         regroup(3)
         e_quantise(2)
         e_quantise(3)
-
-        for i in range(1, B + S2_LAG + 1):
+        for i in range(1, B - 1):
             q_quantise(i - 1)
-            if HEAD_BATCHES <= i < B:
+            if i >= HEAD_BATCHES:
                 new_q_banks(i)
-                stage1(i, IM, 0)
-                stage1(i, RE, 0)
-                stage1(i, IM, 1)
+                stage1(i, IM, (0, 1))
+                stage1(i, RE, (0, 1))
+                stage1(i, IM, (2, 3))
                 q_out(i, IM)
-                stage1(i, RE, 1)
+                stage1(i, RE, (2, 3))
                 q_out(i, RE)
             regroup(i + REGROUP_AHEAD)
             stage2(i - S2_LAG)
@@ -299,3 +343,20 @@ def tile_autoregressivelsa_pa_t_kernel(tc, E_re, E_im, WKQ_re, WKQ_im, out_0, ou
             s_sub_and_store(i - S2_LAG - 1)
             if i > 1:
                 e_quantise(i + QUANT_AHEAD)
+
+        last = B - 1
+        q_quantise(last - 1)
+        new_q_banks(last)
+        stage1(last, IM, (0, 1, 2, 3))
+        q_out(last, IM)
+        stage1(last, RE, (0, 1, 2, 3))
+        s_sub_and_store(last - S2_LAG - 1)
+        q_out(last, RE)
+        q_quantise_part(last, IM)
+        q_quantise_part(last, RE)
+        for b in range(last - S2_LAG, last):
+            stage2(b)
+            s_out(b)
+        for b in range(last - S2_LAG, last):
+            s_sub_and_store(b)
+        stage2_last(last)

@@ -21,7 +21,7 @@ NEG_IM = 2
 FLOPS = 2 * B * (4 * D * D * T + 4 * T * D * T)
 
 LOAD_CHUNKS = [1, 1, 1, 1, 2, 2, 4, 4, 4, 4, 4, 4]
-STORE_GROUPS = [4, 4, 4, 4, 4, 4, 2, 2, 2, 1, 1]
+STORE_GROUPS = [4, 4, 4, 4, 4, 4, 4, 2, 1, 1]
 GROUPS = [1] * 4 + [2] * 13 + [1] * 2
 REGROUP_AHEAD = 3
 QUANT_AHEAD = 2
@@ -220,43 +220,6 @@ def tile_autoregressivelsa_pa_t_kernel(tc, E_re, E_im, WKQ_re, WKQ_im, out_0, ou
                 in_=q_grp[g][:].rearrange("p u t j -> p (u t j)"),
             )
 
-        def q_quantise_part(b, part):
-            g, bb = member[b]
-            n = GROUPS[g]
-            if g not in q_codes:
-                q_codes[g] = qrot.tile([P, 2 * n * T], U32, name="q_codes", tag="q_codes", align_bytes=64)
-                q_scales[g] = qrot.tile([P, 2 * n * T], U8, name="q_scales", tag="q_scales", align_bytes=64)
-            part_cols = cols(2 * bb + part)
-            nc.vector.quantize_mx(
-                out=q_codes[g][:, part_cols].bitcast(FP8X4),
-                scales=q_scales[g][:, part_cols],
-                in_=q_grp[g][:, 2 * bb + part, :, :].rearrange("p t j -> p (t j)"),
-            )
-
-        def stage2_last(b):
-            g, bb = member[b]
-            sg, sbb, n, first_b = group_of[b]
-            xz = outs.tile([P, 2, n, T], F32, name="xz", tag="xz")
-            oim = outs.tile([P, n, T], F32, name="oim", tag="oim")
-            banks = {}
-            for slot, a, q, first, last_pass in [(0, IM, RE, True, True), (2, RE, IM, True, True), (1, RE, RE, True, False), (1, IM, IM, False, True)]:
-                if first:
-                    banks[slot] = pq.tile([P, T], F32, name="last_bank", tag="q")
-                nc.tensor.matmul_mx(
-                    out=banks[slot][:],
-                    lhsT=e_codes[g][:, cols(2 * bb + a)].bitcast(FP8X4),
-                    lhsT_scale=e_scales[g][:, cols(2 * bb + a)],
-                    rhs=q_codes[g][:, cols(2 * bb + q)].bitcast(FP8X4),
-                    rhs_scale=q_scales[g][:, cols(2 * bb + q)],
-                    start=first,
-                    stop=last_pass,
-                )
-            nc.scalar.copy(out=xz[:, 0, 0, :], in_=banks[0][:])
-            nc.scalar.copy(out=xz[:, 1, 0, :], in_=banks[1][:])
-            nc.vector.tensor_sub(out=oim[:, 0, :], in0=banks[2][:], in1=xz[:, 0, 0, :])
-            nc.sync.dma_start(out=out_0[first_b:first_b + n].rearrange("b i j -> i b j"), in_=xz[:, 1, :, :])
-            nc.sync.dma_start(out=out_1[first_b:first_b + n].rearrange("b i j -> i b j"), in_=oim[:])
-
         def stage2(b):
             if b < 0 or b >= B:
                 return
@@ -327,9 +290,9 @@ def tile_autoregressivelsa_pa_t_kernel(tc, E_re, E_im, WKQ_re, WKQ_im, out_0, ou
         regroup(3)
         e_quantise(2)
         e_quantise(3)
-        for i in range(1, B - 1):
+        for i in range(1, B + S2_LAG + 1):
             q_quantise(i - 1)
-            if i >= HEAD_BATCHES:
+            if HEAD_BATCHES <= i < B:
                 new_q_banks(i)
                 stage1(i, IM, (0, 1))
                 stage1(i, RE, (0, 1))
@@ -343,20 +306,3 @@ def tile_autoregressivelsa_pa_t_kernel(tc, E_re, E_im, WKQ_re, WKQ_im, out_0, ou
             s_sub_and_store(i - S2_LAG - 1)
             if i > 1:
                 e_quantise(i + QUANT_AHEAD)
-
-        last = B - 1
-        q_quantise(last - 1)
-        new_q_banks(last)
-        stage1(last, IM, (0, 1, 2, 3))
-        q_out(last, IM)
-        stage1(last, RE, (0, 1, 2, 3))
-        s_sub_and_store(last - S2_LAG - 1)
-        q_out(last, RE)
-        q_quantise_part(last, IM)
-        q_quantise_part(last, RE)
-        for b in range(last - S2_LAG, last):
-            stage2(b)
-            s_out(b)
-        for b in range(last - S2_LAG, last):
-            s_sub_and_store(b)
-        stage2_last(last)

@@ -23,6 +23,7 @@ FLOPS = 2 * B * (4 * D * D * T + 4 * T * D * T)
 LOAD_CHUNKS = [1, 1, 1, 1, 2, 2, 4, 4, 4, 4, 4, 4]
 STORE_GROUPS = [4, 4, 4, 4, 4, 4, 4, 2, 1, 1]
 GROUPS = [1] * 4 + [2] * 13 + [1] * 2
+LATE_Q = 5
 REGROUP_AHEAD = 3
 QUANT_AHEAD = 2
 S2_LAG = 4
@@ -176,8 +177,9 @@ def tile_autoregressivelsa_pa_t_kernel(tc, E_re, E_im, WKQ_re, WKQ_im, out_0, ou
             return slice(a * T, (a + 1) * T)
 
         def new_q_banks(b):
+            pool, tag = (ps, "s") if b == HEAD_BATCHES else (pq, "q")
             for part in (IM, RE):
-                q_bank[(b, part)] = pq.tile([P, PACK, T], F32, name="q_bank", tag="q")
+                q_bank[(b, part)] = pool.tile([P, PACK, T], F32, name="q_bank", tag=tag)
 
         def stage1(b, part, js):
             if part == RE:
@@ -291,7 +293,8 @@ def tile_autoregressivelsa_pa_t_kernel(tc, E_re, E_im, WKQ_re, WKQ_im, out_0, ou
         e_quantise(2)
         e_quantise(3)
         for i in range(1, B + S2_LAG + 1):
-            q_quantise(i - 1)
+            if i >= LATE_Q:
+                q_quantise(i - 1)
             if HEAD_BATCHES <= i < B:
                 new_q_banks(i)
                 stage1(i, IM, (0, 1))
@@ -306,3 +309,5 @@ def tile_autoregressivelsa_pa_t_kernel(tc, E_re, E_im, WKQ_re, WKQ_im, out_0, ou
             s_sub_and_store(i - S2_LAG - 1)
             if i > 1:
                 e_quantise(i + QUANT_AHEAD)
+            if i < LATE_Q:
+                q_quantise(i - 1)

@@ -24,6 +24,8 @@ LOAD_CHUNKS = [1, 1, 1, 1, 2, 2, 4, 4, 4, 4, 4, 4]
 STORE_GROUPS = [4, 4, 4, 4, 4, 4, 4, 2, 1, 1]
 GROUPS = [1] * 4 + [2] * 13 + [1] * 2
 LATE_Q = 5
+E_SHIFT = 128
+E_SCALE_SHIFT = 64
 REGROUP_AHEAD = 3
 QUANT_AHEAD = 2
 S2_LAG = 4
@@ -67,12 +69,17 @@ def tile_autoregressivelsa_pa_t_kernel(tc, E_re, E_im, WKQ_re, WKQ_im, out_0, ou
                 if m != NEG_IM:
                     w_raw[(m, h)] = keep.tile([P, n * D], BF16, name="w_raw%d%d" % (m, h))
                 w_grp[(m, h)] = keep.tile([P, n * D], BF16, name="w_grp%d%d" % (m, h), align_bytes=64)
-                w_codes[(m, h)] = keep.tile([P, n * P], U32, name="w_codes%d%d" % (m, h), align_bytes=64)
-                w_scales[(m, h)] = keep.tile([P, n * P], U8, name="w_scales%d%d" % (m, h), align_bytes=64)
+                w_codes[(m, h)] = keep.tile([P, n * P], U32, name="w_codes%d%d" % (m, h), align_bytes=256)
+                w_scales[(m, h)] = keep.tile([P, n * P], U8, name="w_scales%d%d" % (m, h), align_bytes=256)
                 for jj, j in enumerate(js):
                     w_of[(m, j)] = (h, jj)
-        e_codes = [keep.tile([P, 2 * n * T], U32, name="e_codes%d" % g, align_bytes=64) for g, n in enumerate(GROUPS)]
-        e_scales = [keep.tile([P, 2 * n * T], U8, name="e_scales%d" % g, align_bytes=64) for g, n in enumerate(GROUPS)]
+        e_codes = []
+        e_scales = []
+        for g, n in enumerate(GROUPS):
+            codes = keep.tile([P, E_SHIFT // 4 + 2 * n * T], U32, name="e_codes%d" % g, align_bytes=256)
+            scales = keep.tile([P, E_SCALE_SHIFT + 2 * n * T], U8, name="e_scales%d" % g, align_bytes=256)
+            e_codes.append(codes[:, E_SHIFT // 4:E_SHIFT // 4 + 2 * n * T])
+            e_scales.append(scales[:, E_SCALE_SHIFT:E_SCALE_SHIFT + 2 * n * T])
         where = {}
         chunk_start = [sum(LOAD_CHUNKS[:k]) for k in range(len(LOAD_CHUNKS))]
 
@@ -128,14 +135,14 @@ def tile_autoregressivelsa_pa_t_kernel(tc, E_re, E_im, WKQ_re, WKQ_im, out_0, ou
         def w_transpose_and_copy(m, h):
             n = len(W_PIECES[m][h])
             words = w_raw[(m, h)][:].bitcast(F32).rearrange("p (j q e) -> p j e q", j=n, e=2)
-            bank = ps.tile([P, 2, n, P], F32, name="w_bank", tag="s")
-            for e in range(2):
-                for jj in range(n):
-                    nc.tensor.transpose(bank[:, e, jj, :], words[:, jj, e, :], ident[:])
-            nc.scalar.copy(
-                out=w_grp[(m, h)][:].bitcast(F32).rearrange("p (c e) -> p c e", e=2),
-                in_=bank[:].rearrange("p e jj q -> p (jj q) e"),
-            )
+            for jj in range(n):
+                bank = ps.tile([P, 2, P], F32, name="w_bank", tag="s")
+                for e in range(2):
+                    nc.tensor.transpose(bank[:, e, :], words[:, jj, e, :], ident[:])
+                nc.scalar.copy(
+                    out=w_grp[(m, h)][:, jj * D:(jj + 1) * D].bitcast(F32).rearrange("p (q e) -> p q e", e=2),
+                    in_=bank[:].rearrange("p e q -> p q e"),
+                )
 
         def w_negate(h):
             nc.vector.tensor_scalar_mul(out=w_grp[(NEG_IM, h)][:], in0=w_grp[(IM, h)][:], scalar1=-1.0)
@@ -214,8 +221,8 @@ def tile_autoregressivelsa_pa_t_kernel(tc, E_re, E_im, WKQ_re, WKQ_im, out_0, ou
                 return
             g = ends[b]
             n = GROUPS[g]
-            q_codes[g] = qrot.tile([P, 2 * n * T], U32, name="q_codes", tag="q_codes", align_bytes=64)
-            q_scales[g] = qrot.tile([P, 2 * n * T], U8, name="q_scales", tag="q_scales", align_bytes=64)
+            q_codes[g] = qrot.tile([P, 2 * n * T], U32, name="q_codes", tag="q_codes", align_bytes=256)
+            q_scales[g] = qrot.tile([P, 2 * n * T], U8, name="q_scales", tag="q_scales", align_bytes=256)
             nc.vector.quantize_mx(
                 out=q_codes[g][:].bitcast(FP8X4),
                 scales=q_scales[g][:],
@@ -262,18 +269,18 @@ def tile_autoregressivelsa_pa_t_kernel(tc, E_re, E_im, WKQ_re, WKQ_im, out_0, ou
         regroup(0)
         warm(8)
         w_transpose_and_copy(RE, 0)
-        warm(2)
+        warm(1)
         w_quantise(RE, 0)
         e_quantise(0)
         regroup(1)
         w_transpose_and_copy(IM, 0)
-        warm(2)
+        warm(1)
         w_negate(0)
         w_quantise(IM, 0)
         e_quantise(1)
         w_quantise(NEG_IM, 0)
         w_transpose_and_copy(RE, 1)
-        warm(2)
+        warm(1)
         w_quantise(RE, 1)
         w_transpose_and_copy(IM, 1)
         w_negate(1)

from contextlib import ExitStack

import concourse.mybir as mybir
from concourse.masks import make_identity

F32 = mybir.dt.float32
BF16 = mybir.dt.bfloat16
U32 = mybir.dt.uint32
U8 = mybir.dt.uint8
FP8X4 = mybir.dt.float8_e4m3fn_x4

P = 128
PACK = 4
B = 32
D = 512
T = 128
RE = 0
IM = 1
NEG_IM = 2

FLOPS = 2 * B * (4 * D * D * T + 4 * T * D * T)

LOAD_CHUNKS = [1, 1, 1, 1, 2, 2, 4, 4, 4, 4, 4, 4]
STORE_GROUPS = [4, 4, 4, 4, 4, 4, 4, 2, 1, 1]
GROUPS = [1] * 4 + [2] * 13 + [1] * 2
LATE_Q = 5
E_SHIFT = 128
E_SCALE_SHIFT = 64
REGROUP_AHEAD = 3
QUANT_AHEAD = 2
S2_LAG = 4
VECTOR_HELPS_FROM = 30
SCALAR_REGROUPS = (2,)
HEAD_BATCHES = 2
HALVES = ((0, 1), (2, 3))
W_PIECES = (HALVES, HALVES, HALVES)


def tile_autoregressivelsa_pa_t_kernel(tc, E_re, E_im, WKQ_re, WKQ_im, out_0, out_1):
    nc = tc.nc
    assert sum(LOAD_CHUNKS) == B and sum(STORE_GROUPS) == B and sum(GROUPS) == B
    starts = {}
    ends = {}
    member = {}
    for g, n in enumerate(GROUPS):
        first_b = sum(GROUPS[:g])
        starts[first_b] = g
        ends[first_b + n - 1] = g
        for bb in range(n):
            member[first_b + bb] = (g, bb)
    with ExitStack() as ctx:
        keep = ctx.enter_context(tc.tile_pool(name="keep", bufs=1))
        rot = ctx.enter_context(tc.tile_pool(name="rot", bufs=4))
        qrot = ctx.enter_context(tc.tile_pool(name="qrot", bufs=S2_LAG + 3))
        outs = ctx.enter_context(tc.tile_pool(name="outs", bufs=6))
        pq = ctx.enter_context(tc.psum_pool(name="pq", bufs=4))
        ps = ctx.enter_context(tc.psum_pool(name="ps", bufs=4))
        ctx.enter_context(tc.manual_schedule())

        w_dram = [WKQ_re, WKQ_im]
        w_raw = {}
        w_grp = {}
        w_codes = {}
        w_scales = {}
        w_of = {}
        for m in range(3):
            for h, js in enumerate(W_PIECES[m]):
                n = len(js)
                if m != NEG_IM:
                    w_raw[(m, h)] = keep.tile([P, n * D], BF16, name="w_raw%d%d" % (m, h))
                w_grp[(m, h)] = keep.tile([P, n * D], BF16, name="w_grp%d%d" % (m, h), align_bytes=64)
                w_codes[(m, h)] = keep.tile([P, n * P], U32, name="w_codes%d%d" % (m, h), align_bytes=256)
                w_scales[(m, h)] = keep.tile([P, n * P], U8, name="w_scales%d%d" % (m, h), align_bytes=256)
                for jj, j in enumerate(js):
                    w_of[(m, j)] = (h, jj)
        e_codes = []
        e_scales = []
        for g, n in enumerate(GROUPS):
            codes = keep.tile([P, E_SHIFT // 4 + 2 * n * T], U32, name="e_codes%d" % g, align_bytes=256)
            scales = keep.tile([P, E_SCALE_SHIFT + 2 * n * T], U8, name="e_scales%d" % g, align_bytes=256)
            e_codes.append(codes[:, E_SHIFT // 4:E_SHIFT // 4 + 2 * n * T])
            e_scales.append(scales[:, E_SCALE_SHIFT:E_SCALE_SHIFT + 2 * n * T])
        where = {}
        chunk_start = [sum(LOAD_CHUNKS[:k]) for k in range(len(LOAD_CHUNKS))]

        def load_w(m, h):
            js = W_PIECES[m][h]
            nc.sync.dma_start(
                out=w_raw[(m, h)][:].rearrange("p (j c) -> p j c", j=len(js)),
                in_=w_dram[m].rearrange("(p j) c -> p j c", j=PACK)[:, js[0]:js[0] + len(js), :],
            )

        def load_e(k):
            n = LOAD_CHUNKS[k]
            b0 = chunk_start[k]
            er = keep.tile([P, n, 2, PACK * T], BF16, name="e_raw%d" % k)
            nc.sync.dma_start(out=er[:, :, RE, :], in_=E_re[b0:b0 + n].rearrange("b (p j) t -> p b (j t)", j=PACK))
            nc.sync.dma_start(out=er[:, :, IM, :], in_=E_im[b0:b0 + n].rearrange("b (p j) t -> p b (j t)", j=PACK))
            for bb in range(n):
                where[b0 + bb] = (er, bb)

        load_w(RE, 0)
        load_e(0)
        load_w(IM, 0)
        load_e(1)
        load_w(RE, 1)
        load_w(IM, 1)
        for k in range(2, len(LOAD_CHUNKS)):
            load_e(k)
        zeros = keep.tile([P, 2 * T], BF16, name="zeros")
        nc.vector.memset(zeros[:], 0.0)
        ident = keep.tile([P, P], F32, name="ident")
        make_identity(nc, ident[:])
        warm_bank = pq.tile([P, 2 * T], F32, name="warm_bank", tag="q")

        def warm(n):
            for k in range(n):
                nc.tensor.matmul(warm_bank[:], zeros[:, 0:P], zeros[:], start=True, stop=True)

        e_grp = {}
        q_bank = {}
        q_grp = {}
        q_codes = {}
        q_scales = {}
        s_bank = {}
        group_of = {}
        b0 = 0
        for g, n in enumerate(STORE_GROUPS):
            for bb in range(n):
                group_of[b0 + bb] = (g, bb, n, b0)
            b0 += n
        xz_tiles = {}
        oim_tiles = {}

        def w_transpose_and_copy(m, h):
            n = len(W_PIECES[m][h])
            words = w_raw[(m, h)][:].bitcast(F32).rearrange("p (j q e) -> p j e q", j=n, e=2)
            for jj in range(n):
                bank = ps.tile([P, 2, P], F32, name="w_bank", tag="s")
                for e in range(2):
                    nc.tensor.transpose(bank[:, e, :], words[:, jj, e, :], ident[:])
                nc.scalar.copy(
                    out=w_grp[(m, h)][:, jj * D:(jj + 1) * D].bitcast(F32).rearrange("p (q e) -> p q e", e=2),
                    in_=bank[:].rearrange("p e q -> p q e"),
                )

        def w_negate(h):
            nc.vector.tensor_scalar_mul(out=w_grp[(NEG_IM, h)][:], in0=w_grp[(IM, h)][:], scalar1=-1.0)

        def w_quantise(m, h):
            nc.vector.quantize_mx(out=w_codes[(m, h)][:].bitcast(FP8X4), scales=w_scales[(m, h)][:], in_=w_grp[(m, h)][:])

        def regroup(b):
            if b not in starts:
                return
            g = starts[b]
            n = GROUPS[g]
            er, bb = where[b]
            eg = rot.tile([P, 2 * n, T, PACK], BF16, name="e_grp", tag="e_grp", align_bytes=64)
            e_grp[g] = eg
            if g in SCALAR_REGROUPS:
                for a in range(2 * n):
                    nc.scalar.copy(
                        out=eg[:, a, :, :].rearrange("p (c i) j -> p c j i", i=4),
                        in_=er[:, bb + a // 2, a % 2, :].rearrange("p (j c i) -> p c j i", j=PACK, i=4),
                    )
            else:
                nc.vector.tensor_copy(
                    out=eg[:].rearrange("p u (c i) j -> p u c j i", i=4),
                    in_=er[:, bb:bb + n, :, :].rearrange("p b a (j c i) -> p (b a) c j i", j=PACK, i=4),
                )

        def e_quantise(b):
            if b not in starts:
                return
            g = starts[b]
            nc.vector.quantize_mx(
                out=e_codes[g][:].bitcast(FP8X4),
                scales=e_scales[g][:],
                in_=e_grp[g][:].rearrange("p u t j -> p (u t j)"),
            )

        def cols(a):
            return slice(a * T, (a + 1) * T)

        def new_q_banks(b):
            pool, tag = (ps, "s") if b == HEAD_BATCHES else (pq, "q")
            for part in (IM, RE):
                q_bank[(b, part)] = pool.tile([P, PACK, T], F32, name="q_bank", tag=tag)

        def stage1(b, part, js):
            if part == RE:
                terms = [(RE, RE), (NEG_IM, IM)]
            else:
                terms = [(RE, IM), (IM, RE)]
            g, bb = member[b]
            for j in js:
                for n, (m, a) in enumerate(terms):
                    h, jj = w_of[(m, j)]
                    nc.tensor.matmul_mx(
                        out=q_bank[(b, part)][:, j, :],
                        lhsT=w_codes[(m, h)][:, cols(jj)].bitcast(FP8X4),
                        lhsT_scale=w_scales[(m, h)][:, cols(jj)],
                        rhs=e_codes[g][:, cols(2 * bb + a)].bitcast(FP8X4),
                        rhs_scale=e_scales[g][:, cols(2 * bb + a)],
                        start=(n == 0),
                        stop=(n == 1),
                    )

        def q_out(b, part):
            g, bb = member[b]
            if g not in q_grp:
                q_grp[g] = rot.tile([P, 2 * GROUPS[g], T, PACK], BF16, name="q_grp", tag="q_grp", align_bytes=64)
            if part == RE and b >= VECTOR_HELPS_FROM:
                nc.vector.tensor_copy(out=q_grp[g][:, 2 * bb + part, :, :], in_=q_bank[(b, part)][:].rearrange("p j t -> p t j"))
            else:
                nc.scalar.copy(out=q_grp[g][:, 2 * bb + part, :, :], in_=q_bank[(b, part)][:].rearrange("p j t -> p t j"))

        def q_quantise(b):
            if b not in ends:
                return
            g = ends[b]
            n = GROUPS[g]
            q_codes[g] = qrot.tile([P, 2 * n * T], U32, name="q_codes", tag="q_codes", align_bytes=256)
            q_scales[g] = qrot.tile([P, 2 * n * T], U8, name="q_scales", tag="q_scales", align_bytes=256)
            nc.vector.quantize_mx(
                out=q_codes[g][:].bitcast(FP8X4),
                scales=q_scales[g][:],
                in_=q_grp[g][:].rearrange("p u t j -> p (u t j)"),
            )

        def stage2(b):
            if b < 0 or b >= B:
                return
            g, bb = member[b]
            bank = ps.tile([P, 3, T], F32, name="s_bank", tag="s")
            passes = [(1, RE, RE, 2, True, False), (1, IM, IM, 1, False, True), (0, IM, RE, 1, True, True)]
            for slot, a, q, n, first, last in passes:
                q_cols = slice((2 * bb + q) * T, (2 * bb + q + n) * T)
                nc.tensor.matmul_mx(
                    out=bank[:, slot:slot + n, :].rearrange("p s t -> p (s t)"),
                    lhsT=e_codes[g][:, cols(2 * bb + a)].bitcast(FP8X4),
                    lhsT_scale=e_scales[g][:, cols(2 * bb + a)],
                    rhs=q_codes[g][:, q_cols].bitcast(FP8X4),
                    rhs_scale=q_scales[g][:, q_cols],
                    start=first,
                    stop=last,
                )
            s_bank[b] = bank

        def s_out(b):
            if b < 0 or b >= B:
                return
            g, bb, n, first_b = group_of[b]
            if bb == 0:
                xz_tiles[g] = outs.tile([P, 2, n, T], F32, name="xz", tag="xz")
                oim_tiles[g] = outs.tile([P, n, T], F32, name="oim", tag="oim")
            nc.scalar.copy(out=xz_tiles[g][:, :, bb, :], in_=s_bank[b][:, 0:2, :])

        def s_sub_and_store(b):
            if b < 0 or b >= B:
                return
            g, bb, n, first_b = group_of[b]
            nc.vector.tensor_sub(out=oim_tiles[g][:, bb, :], in0=s_bank[b][:, 2, :], in1=xz_tiles[g][:, 0, bb, :])
            if bb == n - 1:
                nc.sync.dma_start(out=out_0[first_b:first_b + n].rearrange("b i j -> i b j"), in_=xz_tiles[g][:, 1, :, :])
                nc.sync.dma_start(out=out_1[first_b:first_b + n].rearrange("b i j -> i b j"), in_=oim_tiles[g][:])

        regroup(0)
        warm(8)
        w_transpose_and_copy(RE, 0)
        warm(1)
        w_quantise(RE, 0)
        e_quantise(0)
        regroup(1)
        w_transpose_and_copy(IM, 0)
        warm(1)
        w_negate(0)
        w_quantise(IM, 0)
        e_quantise(1)
        w_quantise(NEG_IM, 0)
        w_transpose_and_copy(RE, 1)
        warm(1)
        w_quantise(RE, 1)
        w_transpose_and_copy(IM, 1)
        w_negate(1)
        w_quantise(IM, 1)
        w_quantise(NEG_IM, 1)
        regroup(2)
        for b in range(HEAD_BATCHES):
            new_q_banks(b)
        for js in HALVES:
            for part in (IM, RE):
                for b in range(HEAD_BATCHES):
                    stage1(b, part, js)
        for b in range(HEAD_BATCHES):
            q_out(b, IM)
            q_out(b, RE)
        regroup(3)
        e_quantise(2)
        e_quantise(3)
        for i in range(1, B + S2_LAG + 1):
            if i >= LATE_Q:
                q_quantise(i - 1)
            if HEAD_BATCHES <= i < B:
                new_q_banks(i)
                stage1(i, IM, (0, 1))
                stage1(i, RE, (0, 1))
                stage1(i, IM, (2, 3))
                q_out(i, IM)
                stage1(i, RE, (2, 3))
                q_out(i, RE)
            regroup(i + REGROUP_AHEAD)
            stage2(i - S2_LAG)
            s_out(i - S2_LAG)
            s_sub_and_store(i - S2_LAG - 1)
            if i > 1:
                e_quantise(i + QUANT_AHEAD)
            if i < LATE_Q:
                q_quantise(i - 1)
